import numpy as np
import ml_dtypes


def mxq(x, axis, fmt="e4m3"):
    dtype, down = {"e4m3": (ml_dtypes.float8_e4m3fn, 7), "e5m2": (ml_dtypes.float8_e5m2, 14)}[fmt]
    v = np.moveaxis(np.asarray(x, np.float32).astype(ml_dtypes.bfloat16).astype(np.float64), axis, -1)
    blocks = v.reshape(v.shape[:-1] + (-1, 32))
    amax = np.abs(blocks).max(-1, keepdims=True)
    byte = np.maximum(np.where(amax > 0, np.frexp(amax)[1] - 1 + 127, 0) - down, 1)
    scale = np.exp2(byte - 127.0)
    codes = (blocks / scale).astype(np.float32).astype(dtype).astype(np.float64)
    return np.moveaxis((codes * scale).reshape(v.shape), -1, axis)


WIDE = False


def mx_kscale(k):
    if not WIDE:
        return np.ones(k)
    levels = np.array([20, -20, 10, -10, 0])
    a = np.random.permutation(np.resize(levels, k // 512 * 4)).reshape(k // 512, 4)
    idx = np.arange(k)
    return np.exp2(a[idx // 512, idx % 128 // 32])


BF16 = ml_dtypes.bfloat16


def bf(x):
    return np.asarray(x, np.float32).astype(BF16)


def f64(x):
    return np.asarray(x).astype(np.float64)


B, D_IN, D_H = 512, 1024, 1024


def sigmoid(v):
    return 1.0 / (1.0 + np.exp(-v))


def setup_inputs():
    u = mx_kscale(D_H)

    def w_in():
        return bf(np.random.standard_normal((D_H, D_IN)) * 0.6 / np.sqrt(D_IN))

    def w_rec():
        return bf(np.random.standard_normal((D_H, D_H)) * 0.6 / np.sqrt(D_H))

    def bias():
        return bf(np.random.standard_normal(D_H) * 0.3)

    incoming = bf(np.random.standard_normal((B, D_IN)))
    h = bf(np.random.standard_normal((B, D_H)))
    W_i0 = w_in()
    b_W_i = bias()
    W_c0 = w_in()
    b_W_c = bias()
    U_i = w_rec()
    b_U_i = bias()
    U_c = w_rec()
    b_U_c = bias()
    g = bf(np.random.standard_normal((B, D_H)) * np.exp2(np.random.randint(-12, 1, (B, 1))) * 16.0 * u[None, :])
    I_gate = sigmoid(f64(incoming) @ f64(W_i0).T + f64(b_W_i) + f64(h) @ f64(U_i).T + f64(b_U_i))
    C_head = f64(incoming) @ f64(W_c0).T + f64(b_W_c) + f64(h) @ f64(U_c).T + f64(b_U_c)
    return {"incoming": incoming, "h": h,
            "W_i": bf(f64(W_i0) / u[:, None]), "b_W_i": b_W_i,
            "W_c": bf(f64(W_c0) / u[:, None]), "b_W_c": b_W_c,
            "U_i": U_i, "b_U_i": b_U_i, "U_c": U_c, "b_U_c": b_U_c,
            "I_gate": np.asarray(I_gate, np.float32), "C_head": np.asarray(C_head, np.float32),
            "grad_out": g}


def reference(incoming, h, W_i, b_W_i, W_c, b_W_c, U_i, b_U_i, U_c, b_U_c, I_gate, C_head, grad_out):
    g = f64(grad_out)
    ig = f64(I_gate)
    ch = f64(C_head)
    dzi = g * ch * ig * (1.0 - ig)
    dc = g * ig
    a = mxq(dzi, 1, "e5m2") @ mxq(f64(W_i), 0, "e4m3")
    c = mxq(dc, 1, "e5m2") @ mxq(f64(W_c), 0, "e4m3")
    return a + c

@@ -1,0 +1,158 @@
+from contextlib import ExitStack
+
+import concourse.mybir as mybir
+from concourse.masks import make_identity
+
+F32 = mybir.dt.float32
+BF16 = mybir.dt.bfloat16
+U32 = mybir.dt.uint32
+U8 = mybir.dt.uint8
+E4M3_X4 = mybir.dt.float8_e4m3fn_x4
+E5M2_X4 = mybir.dt.float8_e5m2_x4
+MULT = mybir.AluOpType.mult
+SUBTRACT = mybir.AluOpType.subtract
+
+P = 128
+PACK = 4
+K_PASS = P * PACK
+TOKENS = 512
+FEATURES = 1024
+D_IN = 1024
+N_TILE = 512
+TOKEN_TILES = TOKENS // P
+HALVES = FEATURES // K_PASS
+PARTS = 2 * HALVES
+N_TILES = D_IN // N_TILE
+VECTOR_COLS = 384
+
+FLOPS = 2 * TOKENS * (2 * FEATURES) * D_IN
+BYTES = 2 * FEATURES * D_IN * 2 + 2 * TOKENS * FEATURES * 4 + TOKENS * FEATURES * 2 + TOKENS * D_IN * 4
+
+
+def tile_lstmcell_pa_v_kernel(
+    tc, incoming, h, W_i, b_W_i, W_c, b_W_c, U_i, b_U_i, U_c, b_U_c, I_gate, C_head, grad_out, out
+):
+    nc = tc.nc
+    with ExitStack() as ctx:
+        keep = ctx.enter_context(tc.tile_pool(name="keep", bufs=1))
+        weights_in = ctx.enter_context(tc.tile_pool(name="weights_in", bufs=PARTS))
+        weights_grouped = ctx.enter_context(tc.tile_pool(name="weights_grouped", bufs=2))
+        tokens_in = ctx.enter_context(tc.tile_pool(name="tokens_in", bufs=TOKEN_TILES))
+        products = ctx.enter_context(tc.tile_pool(name="products", bufs=2))
+        quantised = ctx.enter_context(tc.tile_pool(name="quantised", bufs=2))
+        results = ctx.enter_context(tc.tile_pool(name="results", bufs=4))
+        transposed = ctx.enter_context(tc.psum_pool(name="transposed", bufs=4))
+        sums = ctx.enter_context(tc.psum_pool(name="sums", bufs=4))
+
+        identity = keep.tile([P, P], F32)
+        make_identity(nc, identity[:])
+        w_words = keep.tile([P, PARTS, D_IN], U32, align_bytes=64)
+        w_scales = keep.tile([P, PARTS, D_IN], U8, align_bytes=64)
+
+        def load_tokens(m):
+            rows = slice(m * P, (m + 1) * P)
+            g_in = tokens_in.tile([P, FEATURES], BF16)
+            nc.sync.dma_start(out=g_in[:], in_=grad_out[rows, :])
+            gate_in = tokens_in.tile([P, FEATURES], F32)
+            nc.sync.dma_start(out=gate_in[:], in_=I_gate[rows, :])
+            head_in = tokens_in.tile([P, FEATURES], F32)
+            nc.sync.dma_start(out=head_in[:], in_=C_head[rows, :])
+            return g_in, gate_in, head_in
+
+        def load_weights(part):
+            matrix = (W_c, W_i)[part // HALVES]
+            first = (part % HALVES) * K_PASS
+            w_in = weights_in.tile([P, PACK, D_IN], BF16)
+            nc.sync.dma_start(
+                out=w_in[:], in_=matrix[first : first + K_PASS, :].rearrange("(t p) n -> p t n", p=P)
+            )
+            return w_in
+
+        def regroup(copy, grouped, w_in, cols):
+            copy(
+                out=grouped[:, cols, :].rearrange("p (c i) t -> p c t i", i=4),
+                in_=w_in[:, :, cols].rearrange("p t (c i) -> p c t i", i=4),
+            )
+
+        def quantise_weights(part, w_in):
+            grouped = weights_grouped.tile([P, D_IN, PACK], BF16, align_bytes=64)
+            regroup(nc.vector.tensor_copy, grouped, w_in, slice(0, VECTOR_COLS))
+            regroup(nc.scalar.copy, grouped, w_in, slice(VECTOR_COLS, D_IN))
+            for n in range(N_TILES):
+                cols = slice(n * N_TILE, (n + 1) * N_TILE)
+                nc.vector.quantize_mx(
+                    out=w_words[:, part, cols].bitcast(E4M3_X4),
+                    scales=w_scales[:, part, cols],
+                    in_=grouped[:, cols, :].rearrange("p n t -> p (n t)"),
+                )
+
+        def gradients(token_tiles):
+            g_in, gate_in, head_in = token_tiles
+            dc = products.tile([P, FEATURES], F32)
+            slope = products.tile([P, FEATURES], F32)
+            dzi = products.tile([P, FEATURES], F32)
+            d_grouped = quantised.tile([P, PARTS, P, PACK], BF16, align_bytes=64)
+            d_words = quantised.tile([P, PARTS, P], U32, align_bytes=64)
+            d_scales = quantised.tile([P, PARTS, P], U8, align_bytes=64)
+
+            def transpose_and_quantise(source, matrix):
+                for half in range(HALVES):
+                    part = source * HALVES + half
+                    flipped = transposed.tile([P, PACK, P], F32)
+                    for t in range(PACK):
+                        first = half * K_PASS + t * P
+                        nc.tensor.transpose(flipped[:, t, :], matrix[:, first : first + P], identity[:])
+                    nc.scalar.copy(out=d_grouped[:, part, :, :], in_=flipped[:].rearrange("p t r -> p r t"))
+                parts = slice(source * HALVES, (source + 1) * HALVES)
+                nc.vector.quantize_mx(
+                    out=d_words[:, parts, :].rearrange("p q r -> p (q r)").bitcast(E5M2_X4),
+                    scales=d_scales[:, parts, :].rearrange("p q r -> p (q r)"),
+                    in_=d_grouped[:, parts, :, :].rearrange("p q r t -> p (q r t)"),
+                )
+
+            for half in range(HALVES):
+                ks = slice(half * K_PASS, (half + 1) * K_PASS)
+                nc.vector.tensor_tensor(out=dc[:, ks], in0=g_in[:, ks], in1=gate_in[:, ks], op=MULT)
+            transpose_and_quantise(0, dc)
+            for half in range(HALVES):
+                ks = slice(half * K_PASS, (half + 1) * K_PASS)
+                nc.vector.scalar_tensor_tensor(
+                    out=slope[:, ks], in0=gate_in[:, ks], scalar=1.0, in1=head_in[:, ks], op0=SUBTRACT, op1=MULT
+                )
+                nc.vector.scalar_tensor_tensor(
+                    out=dzi[:, ks], in0=dc[:, ks], scalar=-1.0, in1=slope[:, ks], op0=MULT, op1=MULT
+                )
+            transpose_and_quantise(1, dzi)
+            return d_words, d_scales
+
+        def multiply(m, d_words, d_scales):
+            acc = [sums.tile([P, N_TILE], F32, name="acc") for n in range(N_TILES)]
+            for part in range(PARTS):
+                for n in range(N_TILES):
+                    cols = slice(n * N_TILE, (n + 1) * N_TILE)
+                    nc.tensor.matmul_mx(
+                        out=acc[n][:],
+                        lhsT=d_words[:, part, :].bitcast(E5M2_X4),
+                        lhsT_scale=d_scales[:, part, :],
+                        rhs=w_words[:, part, cols].bitcast(E4M3_X4),
+                        rhs_scale=w_scales[:, part, cols],
+                        start=(part == 0),
+                        stop=(part == PARTS - 1),
+                    )
+            for n in range(N_TILES):
+                result = results.tile([P, N_TILE], F32)
+                nc.scalar.copy(out=result[:], in_=acc[n][:])
+                nc.sync.dma_start(out=out[m * P : (m + 1) * P, n * N_TILE : (n + 1) * N_TILE], in_=result[:])
+
+        token_tiles = [load_tokens(0)]
+        w_ins = [load_weights(part) for part in range(PARTS)]
+        for m in range(1, TOKEN_TILES):
+            token_tiles.append(load_tokens(m))
+
+        operands = [gradients(token_tiles[0])]
+        for part in range(PARTS):
+            quantise_weights(part, w_ins[part])
+        for m in range(TOKEN_TILES):
+            if m + 1 < TOKEN_TILES:
+                operands.append(gradients(token_tiles[m + 1]))
+            multiply(m, operands[m][0], operands[m][1])

@@ -39,7 +39,7 @@ def tile_lstmcell_pa_v_kernel(
         weights_grouped = ctx.enter_context(tc.tile_pool(name="weights_grouped", bufs=2))
         tokens_in = ctx.enter_context(tc.tile_pool(name="tokens_in", bufs=TOKEN_TILES))
         products = ctx.enter_context(tc.tile_pool(name="products", bufs=2))
-        quantised = ctx.enter_context(tc.tile_pool(name="quantised", bufs=2))
+        quantised = ctx.enter_context(tc.tile_pool(name="quantised", bufs=3))
         results = ctx.enter_context(tc.tile_pool(name="results", bufs=4))
         transposed = ctx.enter_context(tc.psum_pool(name="transposed", bufs=4))
         sums = ctx.enter_context(tc.psum_pool(name="sums", bufs=4))
@@ -103,12 +103,11 @@ def tile_lstmcell_pa_v_kernel(
                         first = half * K_PASS + t * P
                         nc.tensor.transpose(flipped[:, t, :], matrix[:, first : first + P], identity[:])
                     nc.scalar.copy(out=d_grouped[:, part, :, :], in_=flipped[:].rearrange("p t r -> p r t"))
-                parts = slice(source * HALVES, (source + 1) * HALVES)
-                nc.vector.quantize_mx(
-                    out=d_words[:, parts, :].rearrange("p q r -> p (q r)").bitcast(E5M2_X4),
-                    scales=d_scales[:, parts, :].rearrange("p q r -> p (q r)"),
-                    in_=d_grouped[:, parts, :, :].rearrange("p q r t -> p (q r t)"),
-                )
+                    nc.vector.quantize_mx(
+                        out=d_words[:, part, :].bitcast(E5M2_X4),
+                        scales=d_scales[:, part, :],
+                        in_=d_grouped[:, part, :, :].rearrange("p r t -> p (r t)"),
+                    )
 
             for half in range(HALVES):
                 ks = slice(half * K_PASS, (half + 1) * K_PASS)
@@ -144,15 +143,23 @@ def tile_lstmcell_pa_v_kernel(
                 nc.scalar.copy(out=result[:], in_=acc[n][:])
                 nc.sync.dma_start(out=out[m * P : (m + 1) * P, n * N_TILE : (n + 1) * N_TILE], in_=result[:])
 
+        w_ins = [load_weights(0)]
         token_tiles = [load_tokens(0)]
-        w_ins = [load_weights(part) for part in range(PARTS)]
-        for m in range(1, TOKEN_TILES):
-            token_tiles.append(load_tokens(m))
+        w_ins.append(load_weights(1))
+        token_tiles.append(load_tokens(1))
+        w_ins.append(load_weights(2))
+        w_ins.append(load_weights(3))
+        token_tiles.append(load_tokens(2))
+        token_tiles.append(load_tokens(3))
 
-        operands = [gradients(token_tiles[0])]
-        for part in range(PARTS):
-            quantise_weights(part, w_ins[part])
+        operands = []
+        quantise_weights(0, w_ins[0])
+        operands.append(gradients(token_tiles[0]))
+        quantise_weights(1, w_ins[1])
+        operands.append(gradients(token_tiles[1]))
+        quantise_weights(2, w_ins[2])
+        quantise_weights(3, w_ins[3])
         for m in range(TOKEN_TILES):
-            if m + 1 < TOKEN_TILES:
-                operands.append(gradients(token_tiles[m + 1]))
+            if m + 2 < TOKEN_TILES:
+                operands.append(gradients(token_tiles[m + 2]))
             multiply(m, operands[m][0], operands[m][1])

@@ -14,6 +14,7 @@ SUBTRACT = mybir.AluOpType.subtract
 
 P = 128
 PACK = 4
+PAIR = 2
 K_PASS = P * PACK
 TOKENS = 512
 FEATURES = 1024
@@ -23,7 +24,7 @@ TOKEN_TILES = TOKENS // P
 HALVES = FEATURES // K_PASS
 PARTS = 2 * HALVES
 N_TILES = D_IN // N_TILE
-VECTOR_COLS = 384
+VECTOR_COLS = 112
 
 FLOPS = 2 * TOKENS * (2 * FEATURES) * D_IN
 BYTES = 2 * FEATURES * D_IN * 2 + 2 * TOKENS * FEATURES * 4 + TOKENS * FEATURES * 2 + TOKENS * D_IN * 4
@@ -35,12 +36,13 @@ def tile_lstmcell_pa_v_kernel(
     nc = tc.nc
     with ExitStack() as ctx:
         keep = ctx.enter_context(tc.tile_pool(name="keep", bufs=1))
-        weights_in = ctx.enter_context(tc.tile_pool(name="weights_in", bufs=PARTS))
+        first_weights = ctx.enter_context(tc.tile_pool(name="first_weights", bufs=N_TILES))
+        weights_in = ctx.enter_context(tc.tile_pool(name="weights_in", bufs=PARTS - 1))
         weights_grouped = ctx.enter_context(tc.tile_pool(name="weights_grouped", bufs=2))
         tokens_in = ctx.enter_context(tc.tile_pool(name="tokens_in", bufs=TOKEN_TILES))
-        products = ctx.enter_context(tc.tile_pool(name="products", bufs=2))
-        quantised = ctx.enter_context(tc.tile_pool(name="quantised", bufs=3))
-        results = ctx.enter_context(tc.tile_pool(name="results", bufs=4))
+        products = ctx.enter_context(tc.tile_pool(name="products", bufs=3))
+        quantised = ctx.enter_context(tc.tile_pool(name="quantised", bufs=TOKEN_TILES))
+        results = ctx.enter_context(tc.tile_pool(name="results", bufs=8))
         transposed = ctx.enter_context(tc.psum_pool(name="transposed", bufs=4))
         sums = ctx.enter_context(tc.psum_pool(name="sums", bufs=4))
 
@@ -49,117 +51,272 @@ def tile_lstmcell_pa_v_kernel(
         w_words = keep.tile([P, PARTS, D_IN], U32, align_bytes=64)
         w_scales = keep.tile([P, PARTS, D_IN], U8, align_bytes=64)
 
-        def load_tokens(m):
-            rows = slice(m * P, (m + 1) * P)
-            g_in = tokens_in.tile([P, FEATURES], BF16)
-            nc.sync.dma_start(out=g_in[:], in_=grad_out[rows, :])
-            gate_in = tokens_in.tile([P, FEATURES], F32)
-            nc.sync.dma_start(out=gate_in[:], in_=I_gate[rows, :])
-            head_in = tokens_in.tile([P, FEATURES], F32)
-            nc.sync.dma_start(out=head_in[:], in_=C_head[rows, :])
-            return g_in, gate_in, head_in
+        first_copy = keep.tile([P, 1], F32)
+        nc.scalar.copy(out=first_copy[:], in_=identity[:, 0:1])
+
+        first_in = [first_weights.tile([P, PACK, N_TILE], BF16, name="first_in") for n in range(N_TILES)]
+        other_in = [weights_in.tile([P, PACK, D_IN], BF16, name="other_in") for part in range(1, PARTS)]
+        w_in = [[first_in[n][:] for n in range(N_TILES)]]
+        for tile in other_in:
+            w_in.append([tile[:, :, n * N_TILE : (n + 1) * N_TILE] for n in range(N_TILES)])
+        g_in = [tokens_in.tile([P, FEATURES], BF16, name="g_in") for m in range(TOKEN_TILES)]
+        gate_in = [tokens_in.tile([P, FEATURES], F32, name="gate_in") for m in range(TOKEN_TILES)]
+        head_in = [tokens_in.tile([P, FEATURES], F32, name="head_in") for m in range(TOKEN_TILES)]
+        w_grouped = {}
+        dc = {}
+        slope = {}
+        dzi = {}
+        acc = {}
+        dc_banks = {}
+        dzi_banks = {}
+        d_grouped = [quantised.tile([P, PARTS, P, PACK], BF16, align_bytes=64, name="d_grouped") for m in range(TOKEN_TILES)]
+        d_words = [quantised.tile([P, PARTS, P], U32, align_bytes=64, name="d_words") for m in range(TOKEN_TILES)]
+        d_scales = [quantised.tile([P, PARTS, P], U8, align_bytes=64, name="d_scales") for m in range(TOKEN_TILES)]
+
+        whole = slice(0, FEATURES)
+
+        def half(i):
+            return slice(i * K_PASS, (i + 1) * K_PASS)
+
+        def load_first_weights(n):
+            rows = W_c[0:K_PASS, n * N_TILE : (n + 1) * N_TILE]
+            nc.sync.dma_start(out=first_in[n][:], in_=rows.rearrange("(t p) n -> p t n", p=P))
 
         def load_weights(part):
             matrix = (W_c, W_i)[part // HALVES]
             first = (part % HALVES) * K_PASS
-            w_in = weights_in.tile([P, PACK, D_IN], BF16)
-            nc.sync.dma_start(
-                out=w_in[:], in_=matrix[first : first + K_PASS, :].rearrange("(t p) n -> p t n", p=P)
-            )
-            return w_in
+            rows = matrix[first : first + K_PASS, :]
+            tile = other_in[part - 1]
+            if part < HALVES:
+                nc.sync.dma_start(out=tile[:], in_=rows.rearrange("(t p) n -> p t n", p=P))
+            else:
+                nc.sync.dma_start(
+                    out=tile[:].rearrange("p (u e) n -> p u e n", e=PAIR),
+                    in_=rows.rearrange("(u p e) n -> p u e n", p=P, e=PAIR),
+                )
 
-        def regroup(copy, grouped, w_in, cols):
+        def load(tile, source, m, cols):
+            nc.sync.dma_start(out=tile[m][:, cols], in_=source[m * P : (m + 1) * P, cols])
+
+        def regroup(copy, part, n, first, last):
+            grouped = w_grouped[part][:, n * N_TILE + first : n * N_TILE + last, :]
             copy(
-                out=grouped[:, cols, :].rearrange("p (c i) t -> p c t i", i=4),
-                in_=w_in[:, :, cols].rearrange("p t (c i) -> p c t i", i=4),
+                out=grouped.rearrange("p (c i) t -> p c t i", i=4),
+                in_=w_in[part][n][:, :, first:last].rearrange("p t (c i) -> p c t i", i=4),
             )
 
-        def quantise_weights(part, w_in):
-            grouped = weights_grouped.tile([P, D_IN, PACK], BF16, align_bytes=64)
-            regroup(nc.vector.tensor_copy, grouped, w_in, slice(0, VECTOR_COLS))
-            regroup(nc.scalar.copy, grouped, w_in, slice(VECTOR_COLS, D_IN))
+        def open_weights(part):
+            grouped = weights_grouped.tile([P, D_IN, PACK], BF16, align_bytes=64, name="grouped")
+            w_grouped[part] = grouped
+
+        def regroup_vector(part, n):
+            regroup(nc.vector.tensor_copy, part, n, 0, VECTOR_COLS)
+
+        def regroup_scalar(part, n):
+            regroup(nc.scalar.copy, part, n, VECTOR_COLS, N_TILE)
+
+        def quantise_weights(part, n):
+            cols = slice(n * N_TILE, (n + 1) * N_TILE)
+            nc.vector.quantize_mx(
+                out=w_words[:, part, cols].bitcast(E4M3_X4),
+                scales=w_scales[:, part, cols],
+                in_=w_grouped[part][:, cols, :].rearrange("p n t -> p (n t)"),
+            )
+
+        def open_products(m):
+            new_dc = products.tile([P, FEATURES], F32, name="dc_tile")
+            new_slope = products.tile([P, FEATURES], F32, name="slope_tile")
+            new_dzi = products.tile([P, FEATURES], BF16, align_bytes=64, name="dzi_tile")
+            dc[m], slope[m], dzi[m] = new_dc, new_slope, new_dzi
+
+        def product_dc(m, ks):
+            nc.vector.tensor_tensor(out=dc[m][:, ks], in0=g_in[m][:, ks], in1=gate_in[m][:, ks], op=MULT)
+
+        def product_slope(m, ks):
+            nc.vector.scalar_tensor_tensor(
+                out=slope[m][:, ks], in0=gate_in[m][:, ks], scalar=1.0, in1=head_in[m][:, ks], op0=SUBTRACT, op1=MULT
+            )
+
+        def product_dzi(m, ks):
+            nc.vector.scalar_tensor_tensor(
+                out=dzi[m][:, ks], in0=dc[m][:, ks], scalar=-1.0, in1=slope[m][:, ks], op0=MULT, op1=MULT
+            )
+
+        def transpose_dc(m, i):
+            bank = transposed.tile([P, PACK, P], F32, name="bank")
+            for t in range(PACK):
+                first = i * K_PASS + t * P
+                nc.tensor.transpose(bank[:, t, :], dc[m][:, first : first + P], identity[:])
+            dc_banks[m, i] = bank
+
+        def group_dc(m, i):
+            nc.scalar.copy(out=d_grouped[m][:, i, :, :], in_=dc_banks[m, i][:].rearrange("p t r -> p r t"))
+
+        def transpose_dzi(m, halves):
+            bank = transposed.tile([P, len(halves), PAIR, P], F32, name="bank")
+            words = dzi[m][:].bitcast(F32)
+            for slot, i in enumerate(halves):
+                for u in range(PAIR):
+                    first = (i * PAIR + u) * P
+                    nc.tensor.transpose(bank[:, slot, u, :], words[:, first : first + P], identity[:])
+            dzi_banks[m, halves[0]] = bank
+
+        def group_dzi(m, halves):
+            first = HALVES + halves[0]
+            grouped = d_grouped[m][:, first : first + len(halves), :, :].rearrange("p h r t -> p (h r t)").bitcast(F32)
+            nc.scalar.copy(
+                out=grouped.rearrange("p (h r u) -> p h r u", u=PAIR, r=P),
+                in_=dzi_banks[m, halves[0]][:].rearrange("p h u r -> p h r u"),
+            )
+
+        def quantise(m, first, count):
+            parts = slice(first, first + count)
+            nc.vector.quantize_mx(
+                out=d_words[m][:, parts, :].rearrange("p h r -> p (h r)").bitcast(E5M2_X4),
+                scales=d_scales[m][:, parts, :].rearrange("p h r -> p (h r)"),
+                in_=d_grouped[m][:, parts, :, :].rearrange("p h r t -> p (h r t)"),
+            )
+
+        def multiply(m, part):
+            if part == 0:
+                acc[m] = [sums.tile([P, N_TILE], F32, name="acc_tile") for n in range(N_TILES)]
             for n in range(N_TILES):
                 cols = slice(n * N_TILE, (n + 1) * N_TILE)
-                nc.vector.quantize_mx(
-                    out=w_words[:, part, cols].bitcast(E4M3_X4),
-                    scales=w_scales[:, part, cols],
-                    in_=grouped[:, cols, :].rearrange("p n t -> p (n t)"),
+                nc.tensor.matmul_mx(
+                    out=acc[m][n][:],
+                    lhsT=d_words[m][:, part, :].bitcast(E5M2_X4),
+                    lhsT_scale=d_scales[m][:, part, :],
+                    rhs=w_words[:, part, cols].bitcast(E4M3_X4),
+                    rhs_scale=w_scales[:, part, cols],
+                    start=(part == 0),
+                    stop=(part == PARTS - 1),
                 )
 
-        def gradients(token_tiles):
-            g_in, gate_in, head_in = token_tiles
-            dc = products.tile([P, FEATURES], F32)
-            slope = products.tile([P, FEATURES], F32)
-            dzi = products.tile([P, FEATURES], F32)
-            d_grouped = quantised.tile([P, PARTS, P, PACK], BF16, align_bytes=64)
-            d_words = quantised.tile([P, PARTS, P], U32, align_bytes=64)
-            d_scales = quantised.tile([P, PARTS, P], U8, align_bytes=64)
+        def store(copy, m, n):
+            result = results.tile([P, N_TILE], F32, name="result")
+            copy(out=result[:], in_=acc[m][n][:])
+            nc.sync.dma_start(out=out[m * P : (m + 1) * P, n * N_TILE : (n + 1) * N_TILE], in_=result[:])
 
-            def transpose_and_quantise(source, matrix):
-                for half in range(HALVES):
-                    part = source * HALVES + half
-                    flipped = transposed.tile([P, PACK, P], F32)
-                    for t in range(PACK):
-                        first = half * K_PASS + t * P
-                        nc.tensor.transpose(flipped[:, t, :], matrix[:, first : first + P], identity[:])
-                    nc.scalar.copy(out=d_grouped[:, part, :, :], in_=flipped[:].rearrange("p t r -> p r t"))
-                    nc.vector.quantize_mx(
-                        out=d_words[:, part, :].bitcast(E5M2_X4),
-                        scales=d_scales[:, part, :],
-                        in_=d_grouped[:, part, :, :].rearrange("p r t -> p (r t)"),
-                    )
+        load_first_weights(0)
+        load(g_in, grad_out, 0, whole)
+        load(gate_in, I_gate, 0, half(0))
+        load(gate_in, I_gate, 0, half(1))
+        load_first_weights(1)
+        load(head_in, C_head, 0, whole)
+        load_weights(1)
+        load(g_in, grad_out, 1, whole)
+        load(gate_in, I_gate, 1, whole)
+        load(head_in, C_head, 1, whole)
+        load_weights(2)
+        load(g_in, grad_out, 2, whole)
+        load(gate_in, I_gate, 2, whole)
+        load_weights(3)
+        load(head_in, C_head, 2, whole)
+        load(g_in, grad_out, 3, whole)
+        load(gate_in, I_gate, 3, whole)
+        load(head_in, C_head, 3, whole)
 
-            for half in range(HALVES):
-                ks = slice(half * K_PASS, (half + 1) * K_PASS)
-                nc.vector.tensor_tensor(out=dc[:, ks], in0=g_in[:, ks], in1=gate_in[:, ks], op=MULT)
-            transpose_and_quantise(0, dc)
-            for half in range(HALVES):
-                ks = slice(half * K_PASS, (half + 1) * K_PASS)
-                nc.vector.scalar_tensor_tensor(
-                    out=slope[:, ks], in0=gate_in[:, ks], scalar=1.0, in1=head_in[:, ks], op0=SUBTRACT, op1=MULT
-                )
-                nc.vector.scalar_tensor_tensor(
-                    out=dzi[:, ks], in0=dc[:, ks], scalar=-1.0, in1=slope[:, ks], op0=MULT, op1=MULT
-                )
-            transpose_and_quantise(1, dzi)
-            return d_words, d_scales
-
-        def multiply(m, d_words, d_scales):
-            acc = [sums.tile([P, N_TILE], F32, name="acc") for n in range(N_TILES)]
-            for part in range(PARTS):
-                for n in range(N_TILES):
-                    cols = slice(n * N_TILE, (n + 1) * N_TILE)
-                    nc.tensor.matmul_mx(
-                        out=acc[n][:],
-                        lhsT=d_words[:, part, :].bitcast(E5M2_X4),
-                        lhsT_scale=d_scales[:, part, :],
-                        rhs=w_words[:, part, cols].bitcast(E4M3_X4),
-                        rhs_scale=w_scales[:, part, cols],
-                        start=(part == 0),
-                        stop=(part == PARTS - 1),
-                    )
-            for n in range(N_TILES):
-                result = results.tile([P, N_TILE], F32)
-                nc.scalar.copy(out=result[:], in_=acc[n][:])
-                nc.sync.dma_start(out=out[m * P : (m + 1) * P, n * N_TILE : (n + 1) * N_TILE], in_=result[:])
-
-        w_ins = [load_weights(0)]
-        token_tiles = [load_tokens(0)]
-        w_ins.append(load_weights(1))
-        token_tiles.append(load_tokens(1))
-        w_ins.append(load_weights(2))
-        w_ins.append(load_weights(3))
-        token_tiles.append(load_tokens(2))
-        token_tiles.append(load_tokens(3))
-
-        operands = []
-        quantise_weights(0, w_ins[0])
-        operands.append(gradients(token_tiles[0]))
-        quantise_weights(1, w_ins[1])
-        operands.append(gradients(token_tiles[1]))
-        quantise_weights(2, w_ins[2])
-        quantise_weights(3, w_ins[3])
-        for m in range(TOKEN_TILES):
-            if m + 2 < TOKEN_TILES:
-                operands.append(gradients(token_tiles[m + 2]))
-            multiply(m, operands[m][0], operands[m][1])
+        both = (0, 1)
+        open_weights(0)
+        open_products(0)
+        regroup_scalar(0, 0)
+        regroup_vector(0, 0)
+        product_dc(0, half(0))
+        transpose_dc(0, 0)
+        product_dc(0, half(1))
+        transpose_dc(0, 1)
+        quantise_weights(0, 0)
+        group_dc(0, 0)
+        group_dc(0, 1)
+        regroup_scalar(0, 1)
+        regroup_vector(0, 1)
+        product_slope(0, whole)
+        quantise(0, 0, 2)
+        quantise_weights(0, 1)
+        product_dzi(0, whole)
+        transpose_dzi(0, both)
+        open_weights(1)
+        regroup_scalar(1, 0)
+        regroup_vector(1, 0)
+        regroup_vector(1, 1)
+        quantise_weights(1, 0)
+        group_dzi(0, both)
+        regroup_scalar(1, 1)
+        open_products(1)
+        product_dc(1, whole)
+        transpose_dc(1, 0)
+        transpose_dc(1, 1)
+        product_slope(1, whole)
+        quantise_weights(1, 1)
+        group_dc(1, 0)
+        group_dc(1, 1)
+        quantise(0, 2, 2)
+        product_dzi(1, whole)
+        multiply(0, 0)
+        multiply(0, 1)
+        transpose_dzi(1, both)
+        open_weights(2)
+        regroup_scalar(2, 0)
+        regroup_vector(2, 0)
+        quantise(1, 0, 2)
+        regroup_scalar(2, 1)
+        regroup_vector(2, 1)
+        quantise_weights(2, 0)
+        multiply(1, 0)
+        multiply(1, 1)
+        group_dzi(1, both)
+        open_products(2)
+        product_dc(2, whole)
+        quantise_weights(2, 1)
+        transpose_dc(2, 0)
+        transpose_dc(2, 1)
+        quantise(1, 2, 2)
+        multiply(0, 2)
+        multiply(1, 2)
+        open_weights(3)
+        regroup_scalar(3, 0)
+        regroup_vector(3, 0)
+        group_dc(2, 0)
+        group_dc(2, 1)
+        regroup_scalar(3, 1)
+        regroup_vector(3, 1)
+        quantise_weights(3, 0)
+        product_slope(2, whole)
+        quantise(2, 0, 2)
+        quantise_weights(3, 1)
+        product_dzi(2, whole)
+        multiply(0, 3)
+        multiply(1, 3)
+        transpose_dzi(2, both)
+        group_dzi(2, both)
+        store(nc.scalar.copy, 0, 0)
+        store(nc.scalar.copy, 0, 1)
+        open_products(3)
+        product_dc(3, whole)
+        transpose_dc(3, 0)
+        transpose_dc(3, 1)
+        store(nc.scalar.copy, 1, 0)
+        group_dc(3, 0)
+        group_dc(3, 1)
+        store(nc.scalar.copy, 1, 1)
+        product_slope(3, whole)
+        quantise(2, 2, 2)
+        for part in range(PARTS):
+            multiply(2, part)
+        product_dzi(3, half(0))
+        transpose_dzi(3, (0,))
+        store(nc.scalar.copy, 2, 0)
+        quantise(3, 0, 2)
+        product_dzi(3, half(1))
+        group_dzi(3, (0,))
+        transpose_dzi(3, (1,))
+        store(nc.vector.tensor_copy, 2, 1)
+        group_dzi(3, (1,))
+        quantise(3, 2, 1)
+        multiply(3, 0)
+        multiply(3, 1)
+        multiply(3, 2)
+        quantise(3, 3, 1)
+        multiply(3, 3)
+        store(nc.scalar.copy, 3, 0)
+        store(nc.vector.tensor_copy, 3, 1)

@@ -24,7 +24,7 @@ TOKEN_TILES = TOKENS // P
 HALVES = FEATURES // K_PASS
 PARTS = 2 * HALVES
 N_TILES = D_IN // N_TILE
-VECTOR_COLS = 112
+VECTOR_COLS = 176
 
 FLOPS = 2 * TOKENS * (2 * FEATURES) * D_IN
 BYTES = 2 * FEATURES * D_IN * 2 + 2 * TOKENS * FEATURES * 4 + TOKENS * FEATURES * 2 + TOKENS * D_IN * 4

@@ -113,7 +113,9 @@ def tile_lstmcell_pa_v_kernel(
             regroup(nc.vector.tensor_copy, part, n, 0, VECTOR_COLS)
 
         def regroup_scalar(part, n):
-            regroup(nc.scalar.copy, part, n, VECTOR_COLS, N_TILE)
+            middle = (VECTOR_COLS + N_TILE) // 2
+            regroup(nc.scalar.copy, part, n, VECTOR_COLS, middle)
+            regroup(nc.scalar.copy, part, n, middle, N_TILE)
 
         def quantise_weights(part, n):
             cols = slice(n * N_TILE, (n + 1) * N_TILE)

from contextlib import ExitStack

import concourse.mybir as mybir
from concourse.masks import make_identity

F32 = mybir.dt.float32
BF16 = mybir.dt.bfloat16
U32 = mybir.dt.uint32
U8 = mybir.dt.uint8
E4M3_X4 = mybir.dt.float8_e4m3fn_x4
E5M2_X4 = mybir.dt.float8_e5m2_x4
MULT = mybir.AluOpType.mult
SUBTRACT = mybir.AluOpType.subtract

P = 128
PACK = 4
PAIR = 2
K_PASS = P * PACK
TOKENS = 512
FEATURES = 1024
D_IN = 1024
N_TILE = 512
TOKEN_TILES = TOKENS // P
HALVES = FEATURES // K_PASS
PARTS = 2 * HALVES
N_TILES = D_IN // N_TILE
VECTOR_COLS = 176

FLOPS = 2 * TOKENS * (2 * FEATURES) * D_IN
BYTES = 2 * FEATURES * D_IN * 2 + 2 * TOKENS * FEATURES * 4 + TOKENS * FEATURES * 2 + TOKENS * D_IN * 4


def tile_lstmcell_pa_v_kernel(
    tc, incoming, h, W_i, b_W_i, W_c, b_W_c, U_i, b_U_i, U_c, b_U_c, I_gate, C_head, grad_out, out
):
    nc = tc.nc
    with ExitStack() as ctx:
        keep = ctx.enter_context(tc.tile_pool(name="keep", bufs=1))
        first_weights = ctx.enter_context(tc.tile_pool(name="first_weights", bufs=N_TILES))
        weights_in = ctx.enter_context(tc.tile_pool(name="weights_in", bufs=PARTS - 1))
        weights_grouped = ctx.enter_context(tc.tile_pool(name="weights_grouped", bufs=2))
        tokens_in = ctx.enter_context(tc.tile_pool(name="tokens_in", bufs=TOKEN_TILES))
        products = ctx.enter_context(tc.tile_pool(name="products", bufs=3))
        quantised = ctx.enter_context(tc.tile_pool(name="quantised", bufs=TOKEN_TILES))
        results = ctx.enter_context(tc.tile_pool(name="results", bufs=8))
        transposed = ctx.enter_context(tc.psum_pool(name="transposed", bufs=4))
        sums = ctx.enter_context(tc.psum_pool(name="sums", bufs=4))

        identity = keep.tile([P, P], F32)
        make_identity(nc, identity[:])
        w_words = keep.tile([P, PARTS, D_IN], U32, align_bytes=64)
        w_scales = keep.tile([P, PARTS, D_IN], U8, align_bytes=64)

        first_copy = keep.tile([P, 1], F32)
        nc.scalar.copy(out=first_copy[:], in_=identity[:, 0:1])

        first_in = [first_weights.tile([P, PACK, N_TILE], BF16, name="first_in") for n in range(N_TILES)]
        other_in = [weights_in.tile([P, PACK, D_IN], BF16, name="other_in") for part in range(1, PARTS)]
        w_in = [[first_in[n][:] for n in range(N_TILES)]]
        for tile in other_in:
            w_in.append([tile[:, :, n * N_TILE : (n + 1) * N_TILE] for n in range(N_TILES)])
        g_in = [tokens_in.tile([P, FEATURES], BF16, name="g_in") for m in range(TOKEN_TILES)]
        gate_in = [tokens_in.tile([P, FEATURES], F32, name="gate_in") for m in range(TOKEN_TILES)]
        head_in = [tokens_in.tile([P, FEATURES], F32, name="head_in") for m in range(TOKEN_TILES)]
        w_grouped = {}
        dc = {}
        slope = {}
        dzi = {}
        acc = {}
        dc_banks = {}
        dzi_banks = {}
        d_grouped = [quantised.tile([P, PARTS, P, PACK], BF16, align_bytes=64, name="d_grouped") for m in range(TOKEN_TILES)]
        d_words = [quantised.tile([P, PARTS, P], U32, align_bytes=64, name="d_words") for m in range(TOKEN_TILES)]
        d_scales = [quantised.tile([P, PARTS, P], U8, align_bytes=64, name="d_scales") for m in range(TOKEN_TILES)]

        whole = slice(0, FEATURES)

        def half(i):
            return slice(i * K_PASS, (i + 1) * K_PASS)

        def load_first_weights(n):
            rows = W_c[0:K_PASS, n * N_TILE : (n + 1) * N_TILE]
            nc.sync.dma_start(out=first_in[n][:], in_=rows.rearrange("(t p) n -> p t n", p=P))

        def load_weights(part):
            matrix = (W_c, W_i)[part // HALVES]
            first = (part % HALVES) * K_PASS
            rows = matrix[first : first + K_PASS, :]
            tile = other_in[part - 1]
            if part < HALVES:
                nc.sync.dma_start(out=tile[:], in_=rows.rearrange("(t p) n -> p t n", p=P))
            else:
                nc.sync.dma_start(
                    out=tile[:].rearrange("p (u e) n -> p u e n", e=PAIR),
                    in_=rows.rearrange("(u p e) n -> p u e n", p=P, e=PAIR),
                )

        def load(tile, source, m, cols):
            nc.sync.dma_start(out=tile[m][:, cols], in_=source[m * P : (m + 1) * P, cols])

        def regroup(copy, part, n, first, last):
            grouped = w_grouped[part][:, n * N_TILE + first : n * N_TILE + last, :]
            copy(
                out=grouped.rearrange("p (c i) t -> p c t i", i=4),
                in_=w_in[part][n][:, :, first:last].rearrange("p t (c i) -> p c t i", i=4),
            )

        def open_weights(part):
            grouped = weights_grouped.tile([P, D_IN, PACK], BF16, align_bytes=64, name="grouped")
            w_grouped[part] = grouped

        def regroup_vector(part, n):
            regroup(nc.vector.tensor_copy, part, n, 0, VECTOR_COLS)

        def regroup_scalar(part, n):
            middle = (VECTOR_COLS + N_TILE) // 2
            regroup(nc.scalar.copy, part, n, VECTOR_COLS, middle)
            regroup(nc.scalar.copy, part, n, middle, N_TILE)

        def quantise_weights(part, n):
            cols = slice(n * N_TILE, (n + 1) * N_TILE)
            nc.vector.quantize_mx(
                out=w_words[:, part, cols].bitcast(E4M3_X4),
                scales=w_scales[:, part, cols],
                in_=w_grouped[part][:, cols, :].rearrange("p n t -> p (n t)"),
            )

        def open_products(m):
            new_dc = products.tile([P, FEATURES], F32, name="dc_tile")
            new_slope = products.tile([P, FEATURES], F32, name="slope_tile")
            new_dzi = products.tile([P, FEATURES], BF16, align_bytes=64, name="dzi_tile")
            dc[m], slope[m], dzi[m] = new_dc, new_slope, new_dzi

        def product_dc(m, ks):
            nc.vector.tensor_tensor(out=dc[m][:, ks], in0=g_in[m][:, ks], in1=gate_in[m][:, ks], op=MULT)

        def product_slope(m, ks):
            nc.vector.scalar_tensor_tensor(
                out=slope[m][:, ks], in0=gate_in[m][:, ks], scalar=1.0, in1=head_in[m][:, ks], op0=SUBTRACT, op1=MULT
            )

        def product_dzi(m, ks):
            nc.vector.scalar_tensor_tensor(
                out=dzi[m][:, ks], in0=dc[m][:, ks], scalar=-1.0, in1=slope[m][:, ks], op0=MULT, op1=MULT
            )

        def transpose_dc(m, i):
            bank = transposed.tile([P, PACK, P], F32, name="bank")
            for t in range(PACK):
                first = i * K_PASS + t * P
                nc.tensor.transpose(bank[:, t, :], dc[m][:, first : first + P], identity[:])
            dc_banks[m, i] = bank

        def group_dc(m, i):
            nc.scalar.copy(out=d_grouped[m][:, i, :, :], in_=dc_banks[m, i][:].rearrange("p t r -> p r t"))

        def transpose_dzi(m, halves):
            bank = transposed.tile([P, len(halves), PAIR, P], F32, name="bank")
            words = dzi[m][:].bitcast(F32)
            for slot, i in enumerate(halves):
                for u in range(PAIR):
                    first = (i * PAIR + u) * P
                    nc.tensor.transpose(bank[:, slot, u, :], words[:, first : first + P], identity[:])
            dzi_banks[m, halves[0]] = bank

        def group_dzi(m, halves):
            first = HALVES + halves[0]
            grouped = d_grouped[m][:, first : first + len(halves), :, :].rearrange("p h r t -> p (h r t)").bitcast(F32)
            nc.scalar.copy(
                out=grouped.rearrange("p (h r u) -> p h r u", u=PAIR, r=P),
                in_=dzi_banks[m, halves[0]][:].rearrange("p h u r -> p h r u"),
            )

        def quantise(m, first, count):
            parts = slice(first, first + count)
            nc.vector.quantize_mx(
                out=d_words[m][:, parts, :].rearrange("p h r -> p (h r)").bitcast(E5M2_X4),
                scales=d_scales[m][:, parts, :].rearrange("p h r -> p (h r)"),
                in_=d_grouped[m][:, parts, :, :].rearrange("p h r t -> p (h r t)"),
            )

        def multiply(m, part):
            if part == 0:
                acc[m] = [sums.tile([P, N_TILE], F32, name="acc_tile") for n in range(N_TILES)]
            for n in range(N_TILES):
                cols = slice(n * N_TILE, (n + 1) * N_TILE)
                nc.tensor.matmul_mx(
                    out=acc[m][n][:],
                    lhsT=d_words[m][:, part, :].bitcast(E5M2_X4),
                    lhsT_scale=d_scales[m][:, part, :],
                    rhs=w_words[:, part, cols].bitcast(E4M3_X4),
                    rhs_scale=w_scales[:, part, cols],
                    start=(part == 0),
                    stop=(part == PARTS - 1),
                )

        def store(copy, m, n):
            result = results.tile([P, N_TILE], F32, name="result")
            copy(out=result[:], in_=acc[m][n][:])
            nc.sync.dma_start(out=out[m * P : (m + 1) * P, n * N_TILE : (n + 1) * N_TILE], in_=result[:])

        load_first_weights(0)
        load(g_in, grad_out, 0, whole)
        load(gate_in, I_gate, 0, half(0))
        load(gate_in, I_gate, 0, half(1))
        load_first_weights(1)
        load(head_in, C_head, 0, whole)
        load_weights(1)
        load(g_in, grad_out, 1, whole)
        load(gate_in, I_gate, 1, whole)
        load(head_in, C_head, 1, whole)
        load_weights(2)
        load(g_in, grad_out, 2, whole)
        load(gate_in, I_gate, 2, whole)
        load_weights(3)
        load(head_in, C_head, 2, whole)
        load(g_in, grad_out, 3, whole)
        load(gate_in, I_gate, 3, whole)
        load(head_in, C_head, 3, whole)

        both = (0, 1)
        open_weights(0)
        open_products(0)
        regroup_scalar(0, 0)
        regroup_vector(0, 0)
        product_dc(0, half(0))
        transpose_dc(0, 0)
        product_dc(0, half(1))
        transpose_dc(0, 1)
        quantise_weights(0, 0)
        group_dc(0, 0)
        group_dc(0, 1)
        regroup_scalar(0, 1)
        regroup_vector(0, 1)
        product_slope(0, whole)
        quantise(0, 0, 2)
        quantise_weights(0, 1)
        product_dzi(0, whole)
        transpose_dzi(0, both)
        open_weights(1)
        regroup_scalar(1, 0)
        regroup_vector(1, 0)
        regroup_vector(1, 1)
        quantise_weights(1, 0)
        group_dzi(0, both)
        regroup_scalar(1, 1)
        open_products(1)
        product_dc(1, whole)
        transpose_dc(1, 0)
        transpose_dc(1, 1)
        product_slope(1, whole)
        quantise_weights(1, 1)
        group_dc(1, 0)
        group_dc(1, 1)
        quantise(0, 2, 2)
        product_dzi(1, whole)
        multiply(0, 0)
        multiply(0, 1)
        transpose_dzi(1, both)
        open_weights(2)
        regroup_scalar(2, 0)
        regroup_vector(2, 0)
        quantise(1, 0, 2)
        regroup_scalar(2, 1)
        regroup_vector(2, 1)
        quantise_weights(2, 0)
        multiply(1, 0)
        multiply(1, 1)
        group_dzi(1, both)
        open_products(2)
        product_dc(2, whole)
        quantise_weights(2, 1)
        transpose_dc(2, 0)
        transpose_dc(2, 1)
        quantise(1, 2, 2)
        multiply(0, 2)
        multiply(1, 2)
        open_weights(3)
        regroup_scalar(3, 0)
        regroup_vector(3, 0)
        group_dc(2, 0)
        group_dc(2, 1)
        regroup_scalar(3, 1)
        regroup_vector(3, 1)
        quantise_weights(3, 0)
        product_slope(2, whole)
        quantise(2, 0, 2)
        quantise_weights(3, 1)
        product_dzi(2, whole)
        multiply(0, 3)
        multiply(1, 3)
        transpose_dzi(2, both)
        group_dzi(2, both)
        store(nc.scalar.copy, 0, 0)
        store(nc.scalar.copy, 0, 1)
        open_products(3)
        product_dc(3, whole)
        transpose_dc(3, 0)
        transpose_dc(3, 1)
        store(nc.scalar.copy, 1, 0)
        group_dc(3, 0)
        group_dc(3, 1)
        store(nc.scalar.copy, 1, 1)
        product_slope(3, whole)
        quantise(2, 2, 2)
        for part in range(PARTS):
            multiply(2, part)
        product_dzi(3, half(0))
        transpose_dzi(3, (0,))
        store(nc.scalar.copy, 2, 0)
        quantise(3, 0, 2)
        product_dzi(3, half(1))
        group_dzi(3, (0,))
        transpose_dzi(3, (1,))
        store(nc.vector.tensor_copy, 2, 1)
        group_dzi(3, (1,))
        quantise(3, 2, 1)
        multiply(3, 0)
        multiply(3, 1)
        multiply(3, 2)
        quantise(3, 3, 1)
        multiply(3, 3)
        store(nc.scalar.copy, 3, 0)
        store(nc.vector.tensor_copy, 3, 1)
